import numpy as np
import ml_dtypes

BF16 = ml_dtypes.bfloat16


def bf(x):
    return np.asarray(x, np.float32).astype(BF16)


def f32(x):
    return np.asarray(x, np.float32)


def f64(x):
    return np.asarray(x).astype(np.float64)


def striped(idx):
    return np.tile(idx.reshape(-1, 16).T, (8, 1))


C, S, N, R = 256, 256, 128, 512
DEG = 8.0


def setup_inputs():
    lim = np.sqrt(6.0 / (C + C))
    return {
        "base": f32(np.random.standard_normal((C, S))),
        "x_dst": f32(np.random.standard_normal((C, N))),
        "x_src": bf(np.random.standard_normal((R, C))),
        "adj": bf(np.random.random((R, N)) < DEG / R),
        "w_neigh": bf(np.random.uniform(-lim, lim, (C, C))),
        "b": f32(0.1 * np.random.standard_normal((C, 1))),
        "offs": striped(np.random.permutation(S)[:N]),
    }


def reference(base, x_dst, x_src, adj, w_neigh, b, offs):
    idx = offs[:16].T.reshape(-1)
    a = f64(adj)
    deg = np.maximum(a.sum(axis=0, keepdims=True), 1.0)
    mean = (f64(x_src).T @ a) / deg
    nb = f64(w_neigh).T @ mean + f64(b)
    out = f64(base).copy()
    out[:, idx] = f64(x_dst) + nb
    return out

@@ -1,0 +1,69 @@
+import concourse.mybir as mybir
+
+P = 128
+C, S, N, R = 256, 256, 128, 512
+CB = C // P
+RT = R // P
+
+F32, BF16, U16 = mybir.dt.float32, mybir.dt.bfloat16, mybir.dt.uint16
+
+FLOPS = 2 * R * N + 2 * R * C * N + 2 * C * C * N
+
+
+def tile_graphsage_kernel(tc, base, x_dst, x_src, adj, w_neigh, b, offs, out):
+    nc = tc.nc
+    add, mult, maximum = mybir.AluOpType.add, mybir.AluOpType.mult, mybir.AluOpType.max
+    identity = mybir.ActivationFunctionType.Identity
+
+    with tc.tile_pool(name="held", bufs=1) as held, tc.psum_pool(name="psum", bufs=1) as psum:
+        adj_sb = held.tile([P, RT, N], BF16, name="adj_sb")
+        nc.sync.dma_start(adj_sb[:], adj.rearrange("(p t) j -> p t j", t=RT))
+        src_sb = held.tile([P, RT, C], BF16, name="src_sb")
+        nc.scalar.dma_start(src_sb[:], x_src.rearrange("(p t) k -> p t k", t=RT))
+        w_sb = held.tile([P, CB, C], BF16, name="w_sb")
+        nc.sync.dma_start(w_sb[:], w_neigh.rearrange("(kb p) c -> p kb c", p=P))
+        dst_sb = held.tile([P, CB, N], F32, name="dst_sb")
+        nc.scalar.dma_start(dst_sb[:], x_dst.rearrange("(cb p) j -> p cb j", p=P))
+        offsets = held.tile([P, N // 16], U16, name="offsets")
+        nc.sync.dma_start(offsets[:], offs)
+        bias = [held.tile([P, 1], F32, name=f"bias{cb}") for cb in range(CB)]
+        window = [held.tile([P, S], F32, name=f"window{cb}") for cb in range(CB)]
+        for cb in range(CB):
+            nc.gpsimd.dma_start(bias[cb][:], b[cb * P : (cb + 1) * P, :])
+        nc.sync.dma_start(window[0][:], base[0:P, :])
+        nc.scalar.dma_start(window[1][:], base[P : 2 * P, :])
+
+        ones = held.tile([P, P], BF16, name="ones")
+        nc.vector.memset(ones[:], 1.0)
+        deg_ps = psum.tile([P, N], F32, name="deg_ps")
+        for t in range(RT):
+            nc.tensor.matmul(deg_ps[:], ones[:], adj_sb[:, t, :], start=(t == 0), stop=(t == RT - 1))
+        deg_sb = held.tile([P, N], F32, name="deg_sb")
+        nc.vector.tensor_scalar(deg_sb[:], deg_ps[:], 1.0, None, maximum)
+        inv_deg = held.tile([P, N], F32, name="inv_deg")
+        nc.vector.reciprocal(inv_deg[:], deg_sb[:])
+
+        mean_bf = []
+        for kb in range(CB):
+            agg_ps = psum.tile([P, N], F32, name=f"agg_ps{kb}")
+            for t in range(RT):
+                nc.tensor.matmul(
+                    agg_ps[:], src_sb[:, t, kb * P : (kb + 1) * P], adj_sb[:, t, :],
+                    start=(t == 0), stop=(t == RT - 1),
+                )
+            mean_kb = held.tile([P, N], BF16, name=f"mean_bf{kb}")
+            nc.vector.tensor_tensor(mean_kb[:], agg_ps[:], inv_deg[:], mult)
+            mean_bf.append(mean_kb)
+
+        for cb in range(CB):
+            nb_ps = psum.tile([P, N], F32, name=f"nb_ps{cb}")
+            for kb in range(CB):
+                nc.tensor.matmul(
+                    nb_ps[:], w_sb[:, kb, cb * P : (cb + 1) * P], mean_bf[kb][:],
+                    start=(kb == 0), stop=(kb == CB - 1),
+                )
+            nb_sb = held.tile([P, N], F32, name=f"nb_sb{cb}")
+            nc.scalar.activation(nb_sb[:], nb_ps[:], identity, bias=bias[cb][:])
+            nc.vector.tensor_tensor(window[cb][:].indirect(offsets[:]), dst_sb[:, cb, :], nb_sb[:], add)
+        nc.sync.dma_start(out[0:P, :], window[0][:])
+        nc.scalar.dma_start(out[P : 2 * P, :], window[1][:])

@@ -13,7 +13,6 @@ FLOPS = 2 * R * N + 2 * R * C * N + 2 * C * C * N
 def tile_graphsage_kernel(tc, base, x_dst, x_src, adj, w_neigh, b, offs, out):
     nc = tc.nc
     add, mult, maximum = mybir.AluOpType.add, mybir.AluOpType.mult, mybir.AluOpType.max
-    identity = mybir.ActivationFunctionType.Identity
 
     with tc.tile_pool(name="held", bufs=1) as held, tc.psum_pool(name="psum", bufs=1) as psum:
         adj_sb = held.tile([P, RT, N], BF16, name="adj_sb")
@@ -26,15 +25,16 @@ def tile_graphsage_kernel(tc, base, x_dst, x_src, adj, w_neigh, b, offs, out):
         nc.scalar.dma_start(dst_sb[:], x_dst.rearrange("(cb p) j -> p cb j", p=P))
         offsets = held.tile([P, N // 16], U16, name="offsets")
         nc.sync.dma_start(offsets[:], offs)
-        bias = [held.tile([P, 1], F32, name=f"bias{cb}") for cb in range(CB)]
+        bias_row = held.tile([1, C], F32, name="bias_row")
+        nc.sync.dma_start(bias_row[:], b.rearrange("c o -> o c"))
         window = [held.tile([P, S], F32, name=f"window{cb}") for cb in range(CB)]
-        for cb in range(CB):
-            nc.gpsimd.dma_start(bias[cb][:], b[cb * P : (cb + 1) * P, :])
         nc.sync.dma_start(window[0][:], base[0:P, :])
         nc.scalar.dma_start(window[1][:], base[P : 2 * P, :])
 
         ones = held.tile([P, P], BF16, name="ones")
         nc.vector.memset(ones[:], 1.0)
+        ones_row = held.tile([1, N], F32, name="ones_row")
+        nc.vector.memset(ones_row[:], 1.0)
         deg_ps = psum.tile([P, N], F32, name="deg_ps")
         for t in range(RT):
             nc.tensor.matmul(deg_ps[:], ones[:], adj_sb[:, t, :], start=(t == 0), stop=(t == RT - 1))
@@ -57,13 +57,14 @@ def tile_graphsage_kernel(tc, base, x_dst, x_src, adj, w_neigh, b, offs, out):
 
         for cb in range(CB):
             nb_ps = psum.tile([P, N], F32, name=f"nb_ps{cb}")
+            nc.tensor.matmul(nb_ps[:], bias_row[:, cb * P : (cb + 1) * P], ones_row[:], start=True, stop=False)
             for kb in range(CB):
                 nc.tensor.matmul(
                     nb_ps[:], w_sb[:, kb, cb * P : (cb + 1) * P], mean_bf[kb][:],
-                    start=(kb == 0), stop=(kb == CB - 1),
+                    start=False, stop=(kb == CB - 1),
                 )
             nb_sb = held.tile([P, N], F32, name=f"nb_sb{cb}")
-            nc.scalar.activation(nb_sb[:], nb_ps[:], identity, bias=bias[cb][:])
+            nc.vector.tensor_copy(nb_sb[:], nb_ps[:])
             nc.vector.tensor_tensor(window[cb][:].indirect(offsets[:]), dst_sb[:, cb, :], nb_sb[:], add)
         nc.sync.dma_start(out[0:P, :], window[0][:])
         nc.scalar.dma_start(out[P : 2 * P, :], window[1][:])

@@ -4,6 +4,7 @@ P = 128
 C, S, N, R = 256, 256, 128, 512
 CB = C // P
 RT = R // P
+TH = RT // 2
 
 F32, BF16, U16 = mybir.dt.float32, mybir.dt.bfloat16, mybir.dt.uint16
 
@@ -17,24 +18,24 @@ def tile_graphsage_kernel(tc, base, x_dst, x_src, adj, w_neigh, b, offs, out):
     with tc.tile_pool(name="held", bufs=1) as held, tc.psum_pool(name="psum", bufs=1) as psum:
         adj_sb = held.tile([P, RT, N], BF16, name="adj_sb")
         nc.sync.dma_start(adj_sb[:], adj.rearrange("(p t) j -> p t j", t=RT))
-        src_sb = held.tile([P, RT, C], BF16, name="src_sb")
-        nc.scalar.dma_start(src_sb[:], x_src.rearrange("(p t) k -> p t k", t=RT))
+        src_view = x_src.rearrange("(p t) k -> p t k", t=RT)
+        src_half = [held.tile([P, TH, C], BF16, name=f"src_half{h}") for h in range(2)]
+        nc.scalar.dma_start(src_half[0][:], src_view[:, 0:TH, :])
+        nc.sync.dma_start(src_half[1][:], src_view[:, TH:RT, :])
         w_sb = held.tile([P, CB, C], BF16, name="w_sb")
         nc.sync.dma_start(w_sb[:], w_neigh.rearrange("(kb p) c -> p kb c", p=P))
         dst_sb = held.tile([P, CB, N], F32, name="dst_sb")
         nc.scalar.dma_start(dst_sb[:], x_dst.rearrange("(cb p) j -> p cb j", p=P))
         offsets = held.tile([P, N // 16], U16, name="offsets")
         nc.sync.dma_start(offsets[:], offs)
-        bias_row = held.tile([1, C], F32, name="bias_row")
-        nc.sync.dma_start(bias_row[:], b.rearrange("c o -> o c"))
+        bias = held.tile([P, CB], F32, name="bias")
+        nc.sync.dma_start(bias[:], b.rearrange("(cb p) o -> p (cb o)", p=P))
         window = [held.tile([P, S], F32, name=f"window{cb}") for cb in range(CB)]
         nc.sync.dma_start(window[0][:], base[0:P, :])
         nc.scalar.dma_start(window[1][:], base[P : 2 * P, :])
 
         ones = held.tile([P, P], BF16, name="ones")
         nc.vector.memset(ones[:], 1.0)
-        ones_row = held.tile([1, N], F32, name="ones_row")
-        nc.vector.memset(ones_row[:], 1.0)
         deg_ps = psum.tile([P, N], F32, name="deg_ps")
         for t in range(RT):
             nc.tensor.matmul(deg_ps[:], ones[:], adj_sb[:, t, :], start=(t == 0), stop=(t == RT - 1))
@@ -43,28 +44,34 @@ def tile_graphsage_kernel(tc, base, x_dst, x_src, adj, w_neigh, b, offs, out):
         inv_deg = held.tile([P, N], F32, name="inv_deg")
         nc.vector.reciprocal(inv_deg[:], deg_sb[:])
 
-        mean_bf = []
+        dst_b = held.tile([P, CB, N], F32, name="dst_b")
+        for cb in range(CB):
+            nc.gpsimd.tensor_scalar(dst_b[:, cb, :], dst_sb[:, cb, :], bias[:, cb : cb + 1], None, add)
+
+        total_ps = [psum.tile([P, N], F32, name=f"total_ps{kb}") for kb in range(CB)]
+        total_bf = [held.tile([P, N], BF16, name=f"total_bf{kb}") for kb in range(CB)]
+        for h in range(2):
+            for kb in range(CB):
+                for th in range(TH):
+                    t = h * TH + th
+                    nc.tensor.matmul(
+                        total_ps[kb][:], src_half[h][:, th, kb * P : (kb + 1) * P], adj_sb[:, t, :],
+                        start=(t == 0), stop=(t == RT - 1),
+                    )
+                if h == 1:
+                    nc.scalar.copy(total_bf[kb][:], total_ps[kb][:])
+
+        prod_ps = [psum.tile([P, N], F32, name=f"prod_ps{cb}") for cb in range(CB)]
         for kb in range(CB):
-            agg_ps = psum.tile([P, N], F32, name=f"agg_ps{kb}")
-            for t in range(RT):
+            for cb in range(CB):
                 nc.tensor.matmul(
-                    agg_ps[:], src_sb[:, t, kb * P : (kb + 1) * P], adj_sb[:, t, :],
-                    start=(t == 0), stop=(t == RT - 1),
+                    prod_ps[cb][:], w_sb[:, kb, cb * P : (cb + 1) * P], total_bf[kb][:],
+                    start=(kb == 0), stop=(kb == CB - 1),
                 )
-            mean_kb = held.tile([P, N], BF16, name=f"mean_bf{kb}")
-            nc.vector.tensor_tensor(mean_kb[:], agg_ps[:], inv_deg[:], mult)
-            mean_bf.append(mean_kb)
 
         for cb in range(CB):
-            nb_ps = psum.tile([P, N], F32, name=f"nb_ps{cb}")
-            nc.tensor.matmul(nb_ps[:], bias_row[:, cb * P : (cb + 1) * P], ones_row[:], start=True, stop=False)
-            for kb in range(CB):
-                nc.tensor.matmul(
-                    nb_ps[:], w_sb[:, kb, cb * P : (cb + 1) * P], mean_bf[kb][:],
-                    start=False, stop=(kb == CB - 1),
-                )
             nb_sb = held.tile([P, N], F32, name=f"nb_sb{cb}")
-            nc.vector.tensor_copy(nb_sb[:], nb_ps[:])
-            nc.vector.tensor_tensor(window[cb][:].indirect(offsets[:]), dst_sb[:, cb, :], nb_sb[:], add)
+            nc.vector.tensor_tensor(nb_sb[:], prod_ps[cb][:], inv_deg[:], mult)
+            nc.vector.tensor_tensor(window[cb][:].indirect(offsets[:]), dst_b[:, cb, :], nb_sb[:], add)
         nc.sync.dma_start(out[0:P, :], window[0][:])
         nc.scalar.dma_start(out[P : 2 * P, :], window[1][:])

@@ -20,19 +20,19 @@ def tile_graphsage_kernel(tc, base, x_dst, x_src, adj, w_neigh, b, offs, out):
         nc.sync.dma_start(adj_sb[:], adj.rearrange("(p t) j -> p t j", t=RT))
         src_view = x_src.rearrange("(p t) k -> p t k", t=RT)
         src_half = [held.tile([P, TH, C], BF16, name=f"src_half{h}") for h in range(2)]
-        nc.scalar.dma_start(src_half[0][:], src_view[:, 0:TH, :])
+        nc.sync.dma_start(src_half[0][:], src_view[:, 0:TH, :])
         nc.sync.dma_start(src_half[1][:], src_view[:, TH:RT, :])
         w_sb = held.tile([P, CB, C], BF16, name="w_sb")
         nc.sync.dma_start(w_sb[:], w_neigh.rearrange("(kb p) c -> p kb c", p=P))
-        dst_sb = held.tile([P, CB, N], F32, name="dst_sb")
-        nc.scalar.dma_start(dst_sb[:], x_dst.rearrange("(cb p) j -> p cb j", p=P))
         offsets = held.tile([P, N // 16], U16, name="offsets")
         nc.sync.dma_start(offsets[:], offs)
         bias = held.tile([P, CB], F32, name="bias")
         nc.sync.dma_start(bias[:], b.rearrange("(cb p) o -> p (cb o)", p=P))
+        dst_sb = held.tile([P, CB, N], F32, name="dst_sb")
+        nc.sync.dma_start(dst_sb[:], x_dst.rearrange("(cb p) j -> p cb j", p=P))
         window = [held.tile([P, S], F32, name=f"window{cb}") for cb in range(CB)]
         nc.sync.dma_start(window[0][:], base[0:P, :])
-        nc.scalar.dma_start(window[1][:], base[P : 2 * P, :])
+        nc.sync.dma_start(window[1][:], base[P : 2 * P, :])
 
         ones = held.tile([P, P], BF16, name="ones")
         nc.vector.memset(ones[:], 1.0)

@@ -16,12 +16,14 @@ def tile_graphsage_kernel(tc, base, x_dst, x_src, adj, w_neigh, b, offs, out):
     add, mult, maximum = mybir.AluOpType.add, mybir.AluOpType.mult, mybir.AluOpType.max
 
     with tc.tile_pool(name="held", bufs=1) as held, tc.psum_pool(name="psum", bufs=1) as psum:
-        adj_sb = held.tile([P, RT, N], BF16, name="adj_sb")
-        nc.sync.dma_start(adj_sb[:], adj.rearrange("(p t) j -> p t j", t=RT))
+        adj_view = adj.rearrange("(p t) j -> p t j", t=RT)
+        adj_half = [held.tile([P, TH, N], BF16, name=f"adj_half{h}") for h in range(2)]
         src_view = x_src.rearrange("(p t) k -> p t k", t=RT)
         src_half = [held.tile([P, TH, C], BF16, name=f"src_half{h}") for h in range(2)]
-        nc.sync.dma_start(src_half[0][:], src_view[:, 0:TH, :])
-        nc.sync.dma_start(src_half[1][:], src_view[:, TH:RT, :])
+        for h in range(2):
+            nc.sync.dma_start(adj_half[h][:], adj_view[:, h * TH : (h + 1) * TH, :])
+        for h in range(2):
+            nc.sync.dma_start(src_half[h][:], src_view[:, h * TH : (h + 1) * TH, :])
         w_sb = held.tile([P, CB, C], BF16, name="w_sb")
         nc.sync.dma_start(w_sb[:], w_neigh.rearrange("(kb p) c -> p kb c", p=P))
         offsets = held.tile([P, N // 16], U16, name="offsets")
@@ -38,7 +40,7 @@ def tile_graphsage_kernel(tc, base, x_dst, x_src, adj, w_neigh, b, offs, out):
         nc.vector.memset(ones[:], 1.0)
         deg_ps = psum.tile([P, N], F32, name="deg_ps")
         for t in range(RT):
-            nc.tensor.matmul(deg_ps[:], ones[:], adj_sb[:, t, :], start=(t == 0), stop=(t == RT - 1))
+            nc.tensor.matmul(deg_ps[:], ones[:], adj_half[t // TH][:, t % TH, :], start=(t == 0), stop=(t == RT - 1))
         deg_sb = held.tile([P, N], F32, name="deg_sb")
         nc.vector.tensor_scalar(deg_sb[:], deg_ps[:], 1.0, None, maximum)
         inv_deg = held.tile([P, N], F32, name="inv_deg")
@@ -55,7 +57,7 @@ def tile_graphsage_kernel(tc, base, x_dst, x_src, adj, w_neigh, b, offs, out):
                 for th in range(TH):
                     t = h * TH + th
                     nc.tensor.matmul(
-                        total_ps[kb][:], src_half[h][:, th, kb * P : (kb + 1) * P], adj_sb[:, t, :],
+                        total_ps[kb][:], src_half[h][:, th, kb * P : (kb + 1) * P], adj_half[h][:, th, :],
                         start=(t == 0), stop=(t == RT - 1),
                     )
                 if h == 1:

@@ -14,6 +14,7 @@ FLOPS = 2 * R * N + 2 * R * C * N + 2 * C * C * N
 def tile_graphsage_kernel(tc, base, x_dst, x_src, adj, w_neigh, b, offs, out):
     nc = tc.nc
     add, mult, maximum = mybir.AluOpType.add, mybir.AluOpType.mult, mybir.AluOpType.max
+    identity = mybir.ActivationFunctionType.Identity
 
     with tc.tile_pool(name="held", bufs=1) as held, tc.psum_pool(name="psum", bufs=1) as psum:
         adj_view = adj.rearrange("(p t) j -> p t j", t=RT)
@@ -46,10 +47,6 @@ def tile_graphsage_kernel(tc, base, x_dst, x_src, adj, w_neigh, b, offs, out):
         inv_deg = held.tile([P, N], F32, name="inv_deg")
         nc.vector.reciprocal(inv_deg[:], deg_sb[:])
 
-        dst_b = held.tile([P, CB, N], F32, name="dst_b")
-        for cb in range(CB):
-            nc.gpsimd.tensor_scalar(dst_b[:, cb, :], dst_sb[:, cb, :], bias[:, cb : cb + 1], None, add)
-
         total_ps = [psum.tile([P, N], F32, name=f"total_ps{kb}") for kb in range(CB)]
         total_bf = [held.tile([P, N], BF16, name=f"total_bf{kb}") for kb in range(CB)]
         for h in range(2):
@@ -62,6 +59,10 @@ def tile_graphsage_kernel(tc, base, x_dst, x_src, adj, w_neigh, b, offs, out):
                     )
                 if h == 1:
                     nc.scalar.copy(total_bf[kb][:], total_ps[kb][:])
+
+        dst_b = held.tile([P, CB, N], F32, name="dst_b")
+        for cb in range(CB):
+            nc.scalar.activation(dst_b[:, cb, :], dst_sb[:, cb, :], identity, bias=bias[:, cb : cb + 1])
 
         prod_ps = [psum.tile([P, N], F32, name=f"prod_ps{cb}") for cb in range(CB)]
         for kb in range(CB):
@@ -76,4 +77,4 @@ def tile_graphsage_kernel(tc, base, x_dst, x_src, adj, w_neigh, b, offs, out):
             nc.vector.tensor_tensor(nb_sb[:], prod_ps[cb][:], inv_deg[:], mult)
             nc.vector.tensor_tensor(window[cb][:].indirect(offsets[:]), dst_b[:, cb, :], nb_sb[:], add)
         nc.sync.dma_start(out[0:P, :], window[0][:])
-        nc.scalar.dma_start(out[P : 2 * P, :], window[1][:])
+        nc.sync.dma_start(out[P : 2 * P, :], window[1][:])

@@ -5,6 +5,7 @@ C, S, N, R = 256, 256, 128, 512
 CB = C // P
 RT = R // P
 TH = RT // 2
+TINY = 2.0 ** -60
 
 F32, BF16, U16 = mybir.dt.float32, mybir.dt.bfloat16, mybir.dt.uint16
 
@@ -13,8 +14,9 @@ FLOPS = 2 * R * N + 2 * R * C * N + 2 * C * C * N
 
 def tile_graphsage_kernel(tc, base, x_dst, x_src, adj, w_neigh, b, offs, out):
     nc = tc.nc
-    add, mult, maximum = mybir.AluOpType.add, mybir.AluOpType.mult, mybir.AluOpType.max
+    add, mult = mybir.AluOpType.add, mybir.AluOpType.mult
     identity = mybir.ActivationFunctionType.Identity
+    inverse_root = mybir.ActivationFunctionType.Abs_reciprocal_sqrt
 
     with tc.tile_pool(name="held", bufs=1) as held, tc.psum_pool(name="psum", bufs=1) as psum:
         adj_view = adj.rearrange("(p t) j -> p t j", t=RT)
@@ -39,16 +41,18 @@ def tile_graphsage_kernel(tc, base, x_dst, x_src, adj, w_neigh, b, offs, out):
 
         ones = held.tile([P, P], BF16, name="ones")
         nc.vector.memset(ones[:], 1.0)
+        tiny = held.tile([P, 1], F32, name="tiny")
+        nc.vector.memset(tiny[:], TINY)
         deg_ps = psum.tile([P, N], F32, name="deg_ps")
         for t in range(RT):
             nc.tensor.matmul(deg_ps[:], ones[:], adj_half[t // TH][:, t % TH, :], start=(t == 0), stop=(t == RT - 1))
-        deg_sb = held.tile([P, N], F32, name="deg_sb")
-        nc.vector.tensor_scalar(deg_sb[:], deg_ps[:], 1.0, None, maximum)
+        root = held.tile([P, N], F32, name="root")
+        nc.scalar.activation(root[:], deg_ps[:], inverse_root, bias=tiny[:])
         inv_deg = held.tile([P, N], F32, name="inv_deg")
-        nc.vector.reciprocal(inv_deg[:], deg_sb[:])
+        nc.vector.tensor_tensor(inv_deg[:], root[:], root[:], mult)
 
         total_ps = [psum.tile([P, N], F32, name=f"total_ps{kb}") for kb in range(CB)]
-        total_bf = [held.tile([P, N], BF16, name=f"total_bf{kb}") for kb in range(CB)]
+        mean_bf = [held.tile([P, N], BF16, name=f"mean_bf{kb}") for kb in range(CB)]
         for h in range(2):
             for kb in range(CB):
                 for th in range(TH):
@@ -58,23 +62,20 @@ def tile_graphsage_kernel(tc, base, x_dst, x_src, adj, w_neigh, b, offs, out):
                         start=(t == 0), stop=(t == RT - 1),
                     )
                 if h == 1:
-                    nc.scalar.copy(total_bf[kb][:], total_ps[kb][:])
-
-        dst_b = held.tile([P, CB, N], F32, name="dst_b")
-        for cb in range(CB):
-            nc.scalar.activation(dst_b[:, cb, :], dst_sb[:, cb, :], identity, bias=bias[:, cb : cb + 1])
+                    nc.vector.tensor_tensor(mean_bf[kb][:], total_ps[kb][:], inv_deg[:], mult)
 
         prod_ps = [psum.tile([P, N], F32, name=f"prod_ps{cb}") for cb in range(CB)]
         for kb in range(CB):
             for cb in range(CB):
                 nc.tensor.matmul(
-                    prod_ps[cb][:], w_sb[:, kb, cb * P : (cb + 1) * P], total_bf[kb][:],
+                    prod_ps[cb][:], w_sb[:, kb, cb * P : (cb + 1) * P], mean_bf[kb][:],
                     start=(kb == 0), stop=(kb == CB - 1),
                 )
 
+        nb_sb = [held.tile([P, N], F32, name=f"nb_sb{cb}") for cb in range(CB)]
+        nc.vector.tensor_scalar(nb_sb[0][:], prod_ps[0][:], bias[:, 0:1], None, add)
+        nc.scalar.activation(nb_sb[1][:], prod_ps[1][:], identity, bias=bias[:, 1:2])
         for cb in range(CB):
-            nb_sb = held.tile([P, N], F32, name=f"nb_sb{cb}")
-            nc.vector.tensor_tensor(nb_sb[:], prod_ps[cb][:], inv_deg[:], mult)
-            nc.vector.tensor_tensor(window[cb][:].indirect(offsets[:]), dst_b[:, cb, :], nb_sb[:], add)
+            nc.vector.tensor_tensor(window[cb][:].indirect(offsets[:]), dst_sb[:, cb, :], nb_sb[cb][:], add)
         nc.sync.dma_start(out[0:P, :], window[0][:])
         nc.sync.dma_start(out[P : 2 * P, :], window[1][:])

@@ -31,12 +31,12 @@ def tile_graphsage_kernel(tc, base, x_dst, x_src, adj, w_neigh, b, offs, out):
         nc.sync.dma_start(w_sb[:], w_neigh.rearrange("(kb p) c -> p kb c", p=P))
         offsets = held.tile([P, N // 16], U16, name="offsets")
         nc.sync.dma_start(offsets[:], offs)
-        bias = held.tile([P, CB], F32, name="bias")
-        nc.sync.dma_start(bias[:], b.rearrange("(cb p) o -> p (cb o)", p=P))
         dst_sb = held.tile([P, CB, N], F32, name="dst_sb")
         nc.sync.dma_start(dst_sb[:], x_dst.rearrange("(cb p) j -> p cb j", p=P))
         window = [held.tile([P, S], F32, name=f"window{cb}") for cb in range(CB)]
         nc.sync.dma_start(window[0][:], base[0:P, :])
+        bias = held.tile([P, CB], F32, name="bias")
+        nc.sync.dma_start(bias[:], b.rearrange("(cb p) o -> p (cb o)", p=P))
         nc.sync.dma_start(window[1][:], base[P : 2 * P, :])
 
         ones = held.tile([P, P], BF16, name="ones")

@@ -22,11 +22,11 @@ def tile_graphsage_kernel(tc, base, x_dst, x_src, adj, w_neigh, b, offs, out):
         adj_view = adj.rearrange("(p t) j -> p t j", t=RT)
         adj_half = [held.tile([P, TH, N], BF16, name=f"adj_half{h}") for h in range(2)]
         src_view = x_src.rearrange("(p t) k -> p t k", t=RT)
-        src_half = [held.tile([P, TH, C], BF16, name=f"src_half{h}") for h in range(2)]
+        src_tile = [held.tile([P, C], BF16, name=f"src_tile{t}") for t in range(RT)]
         for h in range(2):
             nc.sync.dma_start(adj_half[h][:], adj_view[:, h * TH : (h + 1) * TH, :])
-        for h in range(2):
-            nc.sync.dma_start(src_half[h][:], src_view[:, h * TH : (h + 1) * TH, :])
+        for t in range(RT):
+            nc.sync.dma_start(src_tile[t][:], src_view[:, t, :])
         w_sb = held.tile([P, CB, C], BF16, name="w_sb")
         nc.sync.dma_start(w_sb[:], w_neigh.rearrange("(kb p) c -> p kb c", p=P))
         offsets = held.tile([P, N // 16], U16, name="offsets")
@@ -58,7 +58,7 @@ def tile_graphsage_kernel(tc, base, x_dst, x_src, adj, w_neigh, b, offs, out):
                 for th in range(TH):
                     t = h * TH + th
                     nc.tensor.matmul(
-                        total_ps[kb][:], src_half[h][:, th, kb * P : (kb + 1) * P], adj_half[h][:, th, :],
+                        total_ps[kb][:], src_tile[t][:, kb * P : (kb + 1) * P], adj_half[h][:, th, :],
                         start=(t == 0), stop=(t == RT - 1),
                     )
                 if h == 1:

@@ -53,16 +53,13 @@ def tile_graphsage_kernel(tc, base, x_dst, x_src, adj, w_neigh, b, offs, out):
 
         total_ps = [psum.tile([P, N], F32, name=f"total_ps{kb}") for kb in range(CB)]
         mean_bf = [held.tile([P, N], BF16, name=f"mean_bf{kb}") for kb in range(CB)]
-        for h in range(2):
-            for kb in range(CB):
-                for th in range(TH):
-                    t = h * TH + th
-                    nc.tensor.matmul(
-                        total_ps[kb][:], src_tile[t][:, kb * P : (kb + 1) * P], adj_half[h][:, th, :],
-                        start=(t == 0), stop=(t == RT - 1),
-                    )
-                if h == 1:
-                    nc.vector.tensor_tensor(mean_bf[kb][:], total_ps[kb][:], inv_deg[:], mult)
+        for kb in range(CB):
+            for t in range(RT):
+                nc.tensor.matmul(
+                    total_ps[kb][:], src_tile[t][:, kb * P : (kb + 1) * P], adj_half[t // TH][:, t % TH, :],
+                    start=(t == 0), stop=(t == RT - 1),
+                )
+            nc.vector.tensor_tensor(mean_bf[kb][:], total_ps[kb][:], inv_deg[:], mult)
 
         prod_ps = [psum.tile([P, N], F32, name=f"prod_ps{cb}") for cb in range(CB)]
         for kb in range(CB):

@@ -27,16 +27,16 @@ def tile_graphsage_kernel(tc, base, x_dst, x_src, adj, w_neigh, b, offs, out):
             nc.sync.dma_start(adj_half[h][:], adj_view[:, h * TH : (h + 1) * TH, :])
         for t in range(RT):
             nc.sync.dma_start(src_tile[t][:], src_view[:, t, :])
-        w_sb = held.tile([P, CB, C], BF16, name="w_sb")
-        nc.sync.dma_start(w_sb[:], w_neigh.rearrange("(kb p) c -> p kb c", p=P))
         offsets = held.tile([P, N // 16], U16, name="offsets")
         nc.sync.dma_start(offsets[:], offs)
+        bias = held.tile([P, CB], F32, name="bias")
+        nc.sync.dma_start(bias[:], b.rearrange("(cb p) o -> p (cb o)", p=P))
+        w_sb = held.tile([P, CB, C], BF16, name="w_sb")
+        nc.sync.dma_start(w_sb[:], w_neigh.rearrange("(kb p) c -> p kb c", p=P))
         dst_sb = held.tile([P, CB, N], F32, name="dst_sb")
         nc.sync.dma_start(dst_sb[:], x_dst.rearrange("(cb p) j -> p cb j", p=P))
         window = [held.tile([P, S], F32, name=f"window{cb}") for cb in range(CB)]
         nc.sync.dma_start(window[0][:], base[0:P, :])
-        bias = held.tile([P, CB], F32, name="bias")
-        nc.sync.dma_start(bias[:], b.rearrange("(cb p) o -> p (cb o)", p=P))
         nc.sync.dma_start(window[1][:], base[P : 2 * P, :])
 
         ones = held.tile([P, P], BF16, name="ones")

@@ -31,13 +31,14 @@ def tile_graphsage_kernel(tc, base, x_dst, x_src, adj, w_neigh, b, offs, out):
         nc.sync.dma_start(offsets[:], offs)
         bias = held.tile([P, CB], F32, name="bias")
         nc.sync.dma_start(bias[:], b.rearrange("(cb p) o -> p (cb o)", p=P))
-        w_sb = held.tile([P, CB, C], BF16, name="w_sb")
-        nc.sync.dma_start(w_sb[:], w_neigh.rearrange("(kb p) c -> p kb c", p=P))
-        dst_sb = held.tile([P, CB, N], F32, name="dst_sb")
-        nc.sync.dma_start(dst_sb[:], x_dst.rearrange("(cb p) j -> p cb j", p=P))
+        w_sb = [held.tile([P, C], BF16, name=f"w_sb{kb}") for kb in range(CB)]
+        for kb in range(CB):
+            nc.sync.dma_start(w_sb[kb][:], w_neigh[kb * P : (kb + 1) * P, :])
+        dst_sb = [held.tile([P, N], F32, name=f"dst_sb{cb}") for cb in range(CB)]
         window = [held.tile([P, S], F32, name=f"window{cb}") for cb in range(CB)]
-        nc.sync.dma_start(window[0][:], base[0:P, :])
-        nc.sync.dma_start(window[1][:], base[P : 2 * P, :])
+        for cb in range(CB):
+            nc.sync.dma_start(dst_sb[cb][:], x_dst[cb * P : (cb + 1) * P, :])
+            nc.sync.dma_start(window[cb][:], base[cb * P : (cb + 1) * P, :])
 
         ones = held.tile([P, P], BF16, name="ones")
         nc.vector.memset(ones[:], 1.0)
@@ -65,7 +66,7 @@ def tile_graphsage_kernel(tc, base, x_dst, x_src, adj, w_neigh, b, offs, out):
         for kb in range(CB):
             for cb in range(CB):
                 nc.tensor.matmul(
-                    prod_ps[cb][:], w_sb[:, kb, cb * P : (cb + 1) * P], mean_bf[kb][:],
+                    prod_ps[cb][:], w_sb[kb][:, cb * P : (cb + 1) * P], mean_bf[kb][:],
                     start=(kb == 0), stop=(kb == CB - 1),
                 )
 
@@ -73,6 +74,6 @@ def tile_graphsage_kernel(tc, base, x_dst, x_src, adj, w_neigh, b, offs, out):
         nc.vector.tensor_scalar(nb_sb[0][:], prod_ps[0][:], bias[:, 0:1], None, add)
         nc.scalar.activation(nb_sb[1][:], prod_ps[1][:], identity, bias=bias[:, 1:2])
         for cb in range(CB):
-            nc.vector.tensor_tensor(window[cb][:].indirect(offsets[:]), dst_sb[:, cb, :], nb_sb[cb][:], add)
+            nc.vector.tensor_tensor(window[cb][:].indirect(offsets[:]), dst_sb[cb][:], nb_sb[cb][:], add)
         nc.sync.dma_start(out[0:P, :], window[0][:])
         nc.sync.dma_start(out[P : 2 * P, :], window[1][:])

import concourse.mybir as mybir

P = 128
C, S, N, R = 256, 256, 128, 512
CB = C // P
RT = R // P
TH = RT // 2
TINY = 2.0 ** -60

F32, BF16, U16 = mybir.dt.float32, mybir.dt.bfloat16, mybir.dt.uint16

FLOPS = 2 * R * N + 2 * R * C * N + 2 * C * C * N


def tile_graphsage_kernel(tc, base, x_dst, x_src, adj, w_neigh, b, offs, out):
    nc = tc.nc
    add, mult = mybir.AluOpType.add, mybir.AluOpType.mult
    identity = mybir.ActivationFunctionType.Identity
    inverse_root = mybir.ActivationFunctionType.Abs_reciprocal_sqrt

    with tc.tile_pool(name="held", bufs=1) as held, tc.psum_pool(name="psum", bufs=1) as psum:
        adj_view = adj.rearrange("(p t) j -> p t j", t=RT)
        adj_half = [held.tile([P, TH, N], BF16, name=f"adj_half{h}") for h in range(2)]
        src_view = x_src.rearrange("(p t) k -> p t k", t=RT)
        src_tile = [held.tile([P, C], BF16, name=f"src_tile{t}") for t in range(RT)]
        for h in range(2):
            nc.sync.dma_start(adj_half[h][:], adj_view[:, h * TH : (h + 1) * TH, :])
        for t in range(RT):
            nc.sync.dma_start(src_tile[t][:], src_view[:, t, :])
        offsets = held.tile([P, N // 16], U16, name="offsets")
        nc.sync.dma_start(offsets[:], offs)
        bias = held.tile([P, CB], F32, name="bias")
        nc.sync.dma_start(bias[:], b.rearrange("(cb p) o -> p (cb o)", p=P))
        w_sb = [held.tile([P, C], BF16, name=f"w_sb{kb}") for kb in range(CB)]
        for kb in range(CB):
            nc.sync.dma_start(w_sb[kb][:], w_neigh[kb * P : (kb + 1) * P, :])
        dst_sb = [held.tile([P, N], F32, name=f"dst_sb{cb}") for cb in range(CB)]
        window = [held.tile([P, S], F32, name=f"window{cb}") for cb in range(CB)]
        for cb in range(CB):
            nc.sync.dma_start(dst_sb[cb][:], x_dst[cb * P : (cb + 1) * P, :])
            nc.sync.dma_start(window[cb][:], base[cb * P : (cb + 1) * P, :])

        ones = held.tile([P, P], BF16, name="ones")
        nc.vector.memset(ones[:], 1.0)
        tiny = held.tile([P, 1], F32, name="tiny")
        nc.vector.memset(tiny[:], TINY)
        deg_ps = psum.tile([P, N], F32, name="deg_ps")
        for t in range(RT):
            nc.tensor.matmul(deg_ps[:], ones[:], adj_half[t // TH][:, t % TH, :], start=(t == 0), stop=(t == RT - 1))
        root = held.tile([P, N], F32, name="root")
        nc.scalar.activation(root[:], deg_ps[:], inverse_root, bias=tiny[:])
        inv_deg = held.tile([P, N], F32, name="inv_deg")
        nc.vector.tensor_tensor(inv_deg[:], root[:], root[:], mult)

        total_ps = [psum.tile([P, N], F32, name=f"total_ps{kb}") for kb in range(CB)]
        mean_bf = [held.tile([P, N], BF16, name=f"mean_bf{kb}") for kb in range(CB)]
        for kb in range(CB):
            for t in range(RT):
                nc.tensor.matmul(
                    total_ps[kb][:], src_tile[t][:, kb * P : (kb + 1) * P], adj_half[t // TH][:, t % TH, :],
                    start=(t == 0), stop=(t == RT - 1),
                )
            nc.vector.tensor_tensor(mean_bf[kb][:], total_ps[kb][:], inv_deg[:], mult)

        prod_ps = [psum.tile([P, N], F32, name=f"prod_ps{cb}") for cb in range(CB)]
        for kb in range(CB):
            for cb in range(CB):
                nc.tensor.matmul(
                    prod_ps[cb][:], w_sb[kb][:, cb * P : (cb + 1) * P], mean_bf[kb][:],
                    start=(kb == 0), stop=(kb == CB - 1),
                )

        nb_sb = [held.tile([P, N], F32, name=f"nb_sb{cb}") for cb in range(CB)]
        nc.vector.tensor_scalar(nb_sb[0][:], prod_ps[0][:], bias[:, 0:1], None, add)
        nc.scalar.activation(nb_sb[1][:], prod_ps[1][:], identity, bias=bias[:, 1:2])
        for cb in range(CB):
            nc.vector.tensor_tensor(window[cb][:].indirect(offsets[:]), dst_sb[cb][:], nb_sb[cb][:], add)
        nc.sync.dma_start(out[0:P, :], window[0][:])
        nc.sync.dma_start(out[P : 2 * P, :], window[1][:])
